import numpy as np
import ml_dtypes


def mxq(x, axis, fmt="e4m3"):
    dtype, down = {"e4m3": (ml_dtypes.float8_e4m3fn, 7), "e5m2": (ml_dtypes.float8_e5m2, 14)}[fmt]
    v = np.moveaxis(np.asarray(x, np.float32).astype(ml_dtypes.bfloat16).astype(np.float64), axis, -1)
    blocks = v.reshape(v.shape[:-1] + (-1, 32))
    amax = np.abs(blocks).max(-1, keepdims=True)
    byte = np.maximum(np.where(amax > 0, np.frexp(amax)[1] - 1 + 127, 0) - down, 1)
    scale = np.exp2(byte - 127.0)
    codes = (blocks / scale).astype(np.float32).astype(dtype).astype(np.float64)
    return np.moveaxis((codes * scale).reshape(v.shape), -1, axis)


WIDE = False


def mx_kscale(k):
    if not WIDE:
        return np.ones(k)
    levels = np.array([10, -10, 5, -5, 0])
    a = np.random.permutation(np.resize(levels, k // 512 * 4)).reshape(k // 512, 4)
    idx = np.arange(k)
    return np.exp2(a[idx // 512, idx % 128 // 32])


BF16 = ml_dtypes.bfloat16


def bf(x):
    return np.asarray(x, np.float32).astype(BF16)


def f64(x):
    return np.asarray(x).astype(np.float64)


B, T, D, H, HD, F = 4, 1024, 512, 8, 64, 128
A = H * HD
EPS = 1e-5
ERF_H = 0.5
ERF_N = 14


def layernorm(x, g, b):
    mu = np.mean(x, axis=-1, keepdims=True)
    var = np.mean(np.square(x - mu), axis=-1, keepdims=True)
    return (x - mu) / np.sqrt(var + EPS) * g + b


def erf(z):
    acc = np.zeros_like(z)
    for n in range(ERF_N):
        tn = (n + 0.5) * ERF_H
        acc = acc + np.exp(-tn * tn) / (tn * tn + z * z)
    return np.tanh(np.pi * z / ERF_H) - 2.0 * ERF_H * z * np.exp(-z * z) / np.pi * acc


def gelu_erf(v):
    return 0.5 * v * (1.0 + erf(v / np.sqrt(2.0)))


def setup_inputs():
    s, t = mx_kscale(A), mx_kscale(D)
    return {"attn": bf(np.random.standard_normal((B, T, A)) * 0.25 * s),
            "x": bf(np.random.standard_normal((B, T, D)) + 0.5 * np.random.standard_normal((B, T, 1))),
            "w_out": bf(np.random.standard_normal((A, D)) * 2.0 / np.sqrt(A) / s[:, None]),
            "b_out": bf(0.1 * np.random.standard_normal(D)),
            "ln2_g": bf((1.0 + 0.1 * np.random.standard_normal(D)) * t),
            "ln2_b": bf(0.1 * np.random.standard_normal(D) * t),
            "w1": bf(np.random.standard_normal((D, F)) / np.sqrt(D) / t[:, None]),
            "b1": bf(0.2 * np.random.standard_normal(F))}


def reference(attn, x, w_out, b_out, ln2_g, ln2_b, w1, b1):
    x_mid = f64(x) + ((mxq(f64(attn), 2, "e4m3") @ mxq(f64(w_out), 0, "e4m3")) + f64(b_out))
    h2 = layernorm(x_mid, f64(ln2_g), f64(ln2_b))
    hid = gelu_erf((mxq(h2, 2, "e4m3") @ mxq(f64(w1), 0, "e4m3")) + f64(b1))
    return x_mid, hid

@@ -1,0 +1,295 @@
+from contextlib import ExitStack
+
+import concourse.mybir as mybir
+from concourse.masks import make_identity
+
+F32 = mybir.dt.float32
+BF16 = mybir.dt.bfloat16
+U32 = mybir.dt.uint32
+U8 = mybir.dt.uint8
+FP8X4 = mybir.dt.float8_e4m3fn_x4
+ALU = mybir.AluOpType
+ACT = mybir.ActivationFunctionType
+
+P = 128
+TOK = 4096
+D = 512
+F = 128
+NT = TOK // P
+EPS = 1e-5
+
+FLOPS = 2 * TOK * D * D + 2 * TOK * D * F
+
+SIZES = (4, 4, 4, 4, 4, 4, 4, 2, 2)
+XB_ON_VECTOR = (0,)
+MANUAL = True
+CA_AHEAD = 3
+XB_AHEAD = 2
+PRE = 2
+OC = 1
+OR = 2
+OE = 3
+
+
+def tile_transformerblock_pb_t_kernel(tc, attn, x, w_out, b_out, ln2_g, ln2_b, w1, b1, out_0, out_1):
+    nc = tc.nc
+    attn_v = attn.flatten_outer_dims().rearrange("(p n) k -> p n k", n=NT)
+    x_v = x.flatten_outer_dims().rearrange("(p n) k -> p n k", n=NT)
+    xmid_v = out_0.flatten_outer_dims().rearrange("(p n) k -> p n k", n=NT)
+    hid_v = out_1.flatten_outer_dims().rearrange("(p n) k -> p n k", n=NT)
+    n_units = len(SIZES)
+    first = [sum(SIZES[:u]) for u in range(n_units)]
+    assert sum(SIZES) == NT
+
+    with ExitStack() as ctx:
+        const = ctx.enter_context(tc.tile_pool(name="const", bufs=1))
+        inp = ctx.enter_context(tc.tile_pool(name="inp", bufs=1))
+        work = ctx.enter_context(tc.tile_pool(name="work", bufs=2))
+        psum = ctx.enter_context(tc.psum_pool(name="psum", bufs=2))
+        if MANUAL:
+            ctx.enter_context(tc.manual_schedule())
+
+        T = {}
+
+        def ok(u):
+            return 0 <= u < n_units
+
+        ident_f = const.tile([P, P], F32)
+        make_identity(nc, ident_f[:])
+        ident_b = const.tile([P, P], BF16)
+        make_identity(nc, ident_b[:])
+
+        crow = const.tile([P, 2 * D], BF16)
+        nc.vector.memset(crow[:], 0.0)
+        grow = const.tile([P, P], BF16)
+        nc.vector.memset(grow[:], 0.0)
+        ones = const.tile([P, P], BF16)
+        nc.vector.memset(ones[:], 1.0)
+        neghalf = const.tile([P, 4], F32)
+        nc.vector.memset(neghalf[:], -0.5)
+        nc.scalar.dma_start(out=crow[0:1, 0:D], in_=b_out.unsqueeze(0))
+        nc.scalar.dma_start(out=crow[0:1, D:D + F], in_=b1.unsqueeze(0))
+        nc.scalar.dma_start(out=grow[0:4, :], in_=ln2_g.rearrange("(t p) -> t p", p=P))
+        nc.scalar.dma_start(out=grow[4:8, :], in_=ln2_b.rearrange("(t p) -> t p", p=P))
+        w1_raw = const.tile([P, 4, F], BF16)
+        nc.scalar.dma_start(out=w1_raw[:], in_=w1.rearrange("(t p) f -> p t f", p=P))
+
+        w_raw = const.tile([P, 4, D], BF16)
+        for u in range(n_units):
+            n = SIZES[u]
+            a_t = inp.tile([P, n, D], BF16, name="attn%d" % u)
+            nc.sync.dma_start(out=a_t[:], in_=attn_v[:, first[u]:first[u] + n, :])
+            T["attn", u] = a_t
+            if u == 0:
+                nc.sync.dma_start(
+                    out=w_raw[:].rearrange("q (u e) d -> q u (e d)", u=2),
+                    in_=w_out.rearrange("(u q e) d -> q u (e d)", u=2, e=2),
+                )
+            x_t = inp.tile([P, n, D], BF16, name="x%d" % u)
+            nc.sync.dma_start(out=x_t[:], in_=x_v[:, first[u]:first[u] + n, :])
+            T["x", u] = x_t
+
+        w_grp = const.tile([P, D, 4], BF16, align_bytes=64)
+        w_codes = const.tile([P, D], U32, align_bytes=64)
+        w_scl = const.tile([P, D], U8, align_bytes=64)
+        w1_grp = const.tile([P, F, 4], BF16, align_bytes=64)
+        w1_codes = const.tile([P, F], U32, align_bytes=64)
+        w1_scl = const.tile([P, F], U8, align_bytes=64)
+        bo_sb = const.tile([P, D], F32)
+        b1_sb = const.tile([P, 4, F], F32)
+        gb = const.tile([P, 8], F32)
+
+        def consts_stage1():
+            nc.vector.tensor_copy(out=w_grp[:].rearrange("q (c i) t -> q c t i", i=4),
+                                  in_=w_raw[:].rearrange("q t (c i) -> q c t i", i=4))
+            bo_ps = psum.tile([P, D], F32, tag="mm2", bufs=1)
+            nc.tensor.matmul(out=bo_ps[:], lhsT=ones[:], rhs=crow[:, 0:D], start=True, stop=True)
+            nc.vector.tensor_copy(out=bo_sb[:], in_=bo_ps[:])
+            nc.vector.quantize_mx(out=w_codes[:].bitcast(FP8X4), scales=w_scl[:],
+                                  in_=w_grp[:].rearrange("q d t -> q (d t)"))
+
+        def consts_stage2():
+            b1_ps = psum.tile([P, D], F32, tag="mm2", bufs=1)
+            nc.tensor.matmul(out=b1_ps[:], lhsT=ones[:], rhs=crow[:, D:2 * D], start=True, stop=True)
+            gb_ps = psum.tile([P, P], BF16, tag="zt", bufs=3)
+            nc.tensor.transpose(gb_ps[:], grow[:], ident_b[:])
+            nc.vector.tensor_copy(out=w1_grp[:], in_=w1_raw[:].rearrange("q t f -> q f t"))
+            nc.vector.tensor_copy(out=b1_sb[:], in_=b1_ps[:, 0:F].unsqueeze(1).to_broadcast([P, 4, F]))
+            nc.vector.tensor_copy(out=gb[:], in_=gb_ps[:, 0:8])
+            nc.vector.quantize_mx(out=w1_codes[:].bitcast(FP8X4), scales=w1_scl[:],
+                                  in_=w1_grp[:].rearrange("q f t -> q (f t)"))
+
+        def st_ta(u):
+            n = SIZES[u]
+            banks = []
+            for h in range((n + 1) // 2):
+                m = min(2, n - 2 * h)
+                tpa = psum.tile([P, D], F32, tag="tpa", bufs=2)
+                for jj in range(m):
+                    words = T["attn", u][:, 2 * h + jj, :].bitcast(F32)
+                    for uu in range(2):
+                        c0 = (2 * jj + uu) * P
+                        nc.tensor.transpose(tpa[:, c0:c0 + P], words[:, uu * P:(uu + 1) * P], ident_f[:])
+                banks.append(tpa)
+            T["tpa", u] = banks
+
+        def st_ca(u):
+            n = SIZES[u]
+            grp1 = work.tile([P, n * P * 4], BF16, align_bytes=64, tag="grp1", bufs=3)
+            T["grp1", u] = grp1
+            g1f = grp1[:].bitcast(F32).rearrange("q (j r u) -> q j r u", j=n, u=2)
+            for h in range((n + 1) // 2):
+                m = min(2, n - 2 * h)
+                nc.scalar.copy(out=g1f[:, 2 * h:2 * h + m, :, :],
+                               in_=T["tpa", u][h][:, 0:m * 2 * P].rearrange("q (j u r) -> q j r u", j=m, u=2))
+
+        def st_q1(u):
+            n = SIZES[u]
+            a_codes = work.tile([P, n * P], U32, align_bytes=64, tag="a_codes", bufs=3)
+            a_scl = work.tile([P, n * P], U8, align_bytes=64, tag="a_scl", bufs=3)
+            nc.vector.quantize_mx(out=a_codes[:].bitcast(FP8X4), scales=a_scl[:], in_=T["grp1", u][:])
+            T["a_codes", u] = a_codes
+            T["a_scl", u] = a_scl
+
+        def st_xm(u):
+            T["xm", u] = work.tile([P, SIZES[u], D], F32, tag="xm", bufs=5, name="xm")
+
+        def st_xb(u, j, eng):
+            eng.tensor_tensor(out=T["xm", u][:, j, :], in0=T["x", u][:, j, :], in1=bo_sb[:], op=ALU.add)
+
+        def st_m1(u, j):
+            mm1 = psum.tile([P, D], F32, tag="mm1", bufs=2)
+            nc.tensor.matmul_mx(out=mm1[:], lhsT=T["a_codes", u][:, j * P:(j + 1) * P].bitcast(FP8X4),
+                                lhsT_scale=T["a_scl", u][:, j * P:(j + 1) * P],
+                                rhs=w_codes[:].bitcast(FP8X4), rhs_scale=w_scl[:], start=True, stop=True)
+            T["mm1", u, j] = mm1
+
+        def st_a(u, j):
+            if j == 0:
+                T["sums", u] = work.tile([P, 4], F32, tag="sums", bufs=4, name="sums")
+            xm = T["xm", u]
+            nc.vector.scalar_tensor_tensor(out=xm[:, j, :], in0=T["mm1", u, j][:], scalar=0.0, in1=xm[:, j, :],
+                                           op0=ALU.add, op1=ALU.add, accum_out=T["sums", u][:, j:j + 1])
+
+        def st_nm(u):
+            n = SIZES[u]
+            negmean = work.tile([P, 4], F32, tag="negmean", bufs=4)
+            nc.vector.tensor_scalar_mul(out=negmean[:, 0:n], in0=T["sums", u][:, 0:n], scalar1=-1.0 / D)
+            T["negmean", u] = negmean
+            nc.sync.dma_start(out=xmid_v[:, first[u]:first[u] + n, :], in_=T["xm", u][:])
+
+        def st_b(u):
+            ssq = work.tile([P, 4], F32, tag="ssq", bufs=4)
+            T["ssq", u] = ssq
+            for j in range(SIZES[u]):
+                junk = work.tile([P, D], BF16, tag="junk", bufs=2)
+                nc.scalar.activation(out=junk[:], in_=T["xm", u][:, j, :], func=ACT.Square,
+                                     bias=T["negmean", u][:, j:j + 1], scale=1.0, accum_out=ssq[:, j:j + 1])
+
+        def st_pow(u):
+            n = SIZES[u]
+            var = work.tile([P, 4], F32, tag="var", bufs=4)
+            nc.gpsimd.tensor_scalar(out=var[:, 0:n], in0=T["ssq", u][:, 0:n], scalar1=1.0 / D, scalar2=EPS,
+                                    op0=ALU.mult, op1=ALU.add)
+            rstd = work.tile([P, 4], F32, tag="rstd", bufs=4)
+            nc.gpsimd.tensor_tensor(out=rstd[:, 0:n], in0=var[:, 0:n], in1=neghalf[:, 0:n], op=ALU.pow)
+            T["rstd", u] = rstd
+
+        def st_c(u):
+            n = SIZES[u]
+            z = work.tile([P, n, D], F32, tag="z", bufs=2)
+            T["z", u] = z
+            for j in range(n):
+                nc.vector.tensor_scalar(out=z[:, j, :], in0=T["xm", u][:, j, :], scalar1=T["negmean", u][:, j:j + 1],
+                                        scalar2=T["rstd", u][:, j:j + 1], op0=ALU.add, op1=ALU.mult)
+
+        def st_tz_d(u):
+            n = SIZES[u]
+            per_bank = 4 // n
+            planes = work.tile([P, 4, n * P], BF16, tag="planes", bufs=2)
+            T["planes", u] = planes
+            zt = None
+            for t in range(4):
+                if t % per_bank == 0:
+                    zt = psum.tile([P, D], F32, tag="zt", bufs=3)
+                c0 = (t % per_bank) * n * P
+                for j in range(n):
+                    nc.tensor.transpose(zt[:, c0 + j * P:c0 + (j + 1) * P], T["z", u][:, j, t * P:(t + 1) * P],
+                                        ident_f[:])
+                nc.scalar.activation(out=planes[:, t, :], in_=zt[:, c0:c0 + n * P], func=ACT.Identity,
+                                     bias=gb[:, 4 + t:5 + t], scale=gb[:, t:t + 1])
+
+        def st_r(u):
+            n = SIZES[u]
+            grp2 = work.tile([P, n * P, 4], BF16, align_bytes=64, tag="grp2", bufs=2)
+            T["grp2", u] = grp2
+            nc.vector.tensor_copy(out=grp2[:].rearrange("p (c i) t -> p c t i", i=4),
+                                  in_=T["planes", u][:].rearrange("p t (c i) -> p c t i", i=4))
+
+        def st_q2(u):
+            n = SIZES[u]
+            h_codes = work.tile([P, n * P], U32, align_bytes=64, tag="h_codes", bufs=2)
+            h_scl = work.tile([P, n * P], U8, align_bytes=64, tag="h_scl", bufs=2)
+            nc.vector.quantize_mx(out=h_codes[:].bitcast(FP8X4), scales=h_scl[:],
+                                  in_=T["grp2", u][:].rearrange("p r t -> p (r t)"))
+            T["h_codes", u] = h_codes
+            T["h_scl", u] = h_scl
+
+        def st_m2(u):
+            n = SIZES[u]
+            mm2 = psum.tile([P, n, F], F32, tag="mm2", bufs=1)
+            T["mm2", u] = mm2
+            for j in range(n):
+                nc.tensor.matmul_mx(out=mm2[:, j, :], lhsT=T["h_codes", u][:, j * P:(j + 1) * P].bitcast(FP8X4),
+                                    lhsT_scale=T["h_scl", u][:, j * P:(j + 1) * P],
+                                    rhs=w1_codes[:].bitcast(FP8X4), rhs_scale=w1_scl[:], start=True, stop=True)
+
+        def st_e(u):
+            n = SIZES[u]
+            pre = work.tile([P, n, F], F32, tag="pre", bufs=2)
+            nc.vector.tensor_tensor(out=pre[:], in0=T["mm2", u][:], in1=b1_sb[:, 0:n, :], op=ALU.add)
+            hid = work.tile([P, n, F], F32, tag="hid", bufs=3)
+            nc.scalar.activation(out=hid[:], in_=pre[:], func=ACT.Gelu)
+            nc.sync.dma_start(out=hid_v[:, first[u]:first[u] + n, :], in_=hid[:])
+
+        for s in range(-CA_AHEAD, n_units + OE + 1):
+            if ok(s - 1):
+                st_pow(s - 1)
+            if ok(s + XB_AHEAD):
+                st_xm(s + XB_AHEAD)
+                if s + XB_AHEAD not in XB_ON_VECTOR:
+                    for j in range(SIZES[s + XB_AHEAD]):
+                        st_xb(s + XB_AHEAD, j, nc.gpsimd)
+            if ok(s):
+                for j in range(SIZES[s]):
+                    if s in XB_ON_VECTOR:
+                        st_xb(s, j, nc.vector)
+                    st_a(s, j)
+                    if j + PRE < SIZES[s]:
+                        st_m1(s, j + PRE)
+                st_nm(s)
+            if ok(s + 1):
+                st_q1(s + 1)
+                for j in range(min(PRE, SIZES[s + 1])):
+                    st_m1(s + 1, j)
+            if ok(s - OE):
+                st_m2(s - OE)
+            if ok(s):
+                st_b(s)
+            if s == 0:
+                consts_stage2()
+            if ok(s - OC):
+                st_c(s - OC)
+                st_tz_d(s - OC)
+            if ok(s + CA_AHEAD):
+                st_ta(s + CA_AHEAD)
+            if s == -CA_AHEAD:
+                consts_stage1()
+            if ok(s - OR):
+                st_r(s - OR)
+            if ok(s - OE):
+                st_e(s - OE)
+            if ok(s - OR):
+                st_q2(s - OR)
+            if ok(s + CA_AHEAD):
+                st_ca(s + CA_AHEAD)

@@ -21,7 +21,7 @@ EPS = 1e-5
 FLOPS = 2 * TOK * D * D + 2 * TOK * D * F
 
 SIZES = (4, 4, 4, 4, 4, 4, 4, 2, 2)
-XB_ON_VECTOR = (0,)
+XB_ON_VECTOR = (0, 1, 2, 3, 4, 5, 6, 7, 8)
 MANUAL = True
 CA_AHEAD = 3
 XB_AHEAD = 2

@@ -21,7 +21,7 @@ EPS = 1e-5
 FLOPS = 2 * TOK * D * D + 2 * TOK * D * F
 
 SIZES = (4, 4, 4, 4, 4, 4, 4, 2, 2)
-XB_ON_VECTOR = (0, 1, 2, 3, 4, 5, 6, 7, 8)
+XB_ON_VECTOR = (0,)
 MANUAL = True
 CA_AHEAD = 3
 XB_AHEAD = 2
@@ -258,11 +258,11 @@ def tile_transformerblock_pb_t_kernel(tc, attn, x, w_out, b_out, ln2_g, ln2_b, w
             if ok(s + XB_AHEAD):
                 st_xm(s + XB_AHEAD)
                 if s + XB_AHEAD not in XB_ON_VECTOR:
-                    for j in range(SIZES[s + XB_AHEAD]):
+                    for j in range(SIZES[s + XB_AHEAD] - 1):
                         st_xb(s + XB_AHEAD, j, nc.gpsimd)
             if ok(s):
                 for j in range(SIZES[s]):
-                    if s in XB_ON_VECTOR:
+                    if s in XB_ON_VECTOR or j == SIZES[s] - 1:
                         st_xb(s, j, nc.vector)
                     st_a(s, j)
                     if j + PRE < SIZES[s]:

@@ -20,15 +20,10 @@ EPS = 1e-5
 
 FLOPS = 2 * TOK * D * D + 2 * TOK * D * F
 
-SIZES = (4, 4, 4, 4, 4, 4, 4, 2, 2)
-XB_ON_VECTOR = (0,)
+SIZES = (2, 4, 4, 4, 4, 4, 4, 4, 2)
 MANUAL = True
 CA_AHEAD = 3
 XB_AHEAD = 2
-PRE = 2
-OC = 1
-OR = 2
-OE = 3
 
 
 def tile_transformerblock_pb_t_kernel(tc, attn, x, w_out, b_out, ln2_g, ln2_b, w1, b1, out_0, out_1):
@@ -67,12 +62,15 @@ def tile_transformerblock_pb_t_kernel(tc, attn, x, w_out, b_out, ln2_g, ln2_b, w
         nc.vector.memset(ones[:], 1.0)
         neghalf = const.tile([P, 4], F32)
         nc.vector.memset(neghalf[:], -0.5)
+        warm = const.tile([P, 2], F32)
+        nc.vector.memset(warm[:], 0.0)
         nc.scalar.dma_start(out=crow[0:1, 0:D], in_=b_out.unsqueeze(0))
+        w1_raw = const.tile([P, 4, F], BF16)
+        nc.scalar.dma_start(out=w1_raw[:], in_=w1.rearrange("(t p) f -> p t f", p=P))
         nc.scalar.dma_start(out=crow[0:1, D:D + F], in_=b1.unsqueeze(0))
         nc.scalar.dma_start(out=grow[0:4, :], in_=ln2_g.rearrange("(t p) -> t p", p=P))
         nc.scalar.dma_start(out=grow[4:8, :], in_=ln2_b.rearrange("(t p) -> t p", p=P))
-        w1_raw = const.tile([P, 4, F], BF16)
-        nc.scalar.dma_start(out=w1_raw[:], in_=w1.rearrange("(t p) f -> p t f", p=P))
+        nc.scalar.activation(out=warm[:, 1:2], in_=warm[:, 0:1], func=ACT.Gelu)
 
         w_raw = const.tile([P, 4, D], BF16)
         for u in range(n_units):
@@ -99,32 +97,31 @@ def tile_transformerblock_pb_t_kernel(tc, attn, x, w_out, b_out, ln2_g, ln2_b, w
         b1_sb = const.tile([P, 4, F], F32)
         gb = const.tile([P, 8], F32)
 
-        def consts_stage1():
-            nc.vector.tensor_copy(out=w_grp[:].rearrange("q (c i) t -> q c t i", i=4),
-                                  in_=w_raw[:].rearrange("q t (c i) -> q c t i", i=4))
-            bo_ps = psum.tile([P, D], F32, tag="mm2", bufs=1)
-            nc.tensor.matmul(out=bo_ps[:], lhsT=ones[:], rhs=crow[:, 0:D], start=True, stop=True)
-            nc.vector.tensor_copy(out=bo_sb[:], in_=bo_ps[:])
-            nc.vector.quantize_mx(out=w_codes[:].bitcast(FP8X4), scales=w_scl[:],
-                                  in_=w_grp[:].rearrange("q d t -> q (d t)"))
+        bo_ps = psum.tile([P, D], F32, tag="mm1", bufs=4)
+        nc.tensor.matmul(out=bo_ps[:], lhsT=ones[:], rhs=crow[:, 0:D], start=True, stop=True)
+        nc.scalar.copy(out=bo_sb[:], in_=bo_ps[:])
+        nc.vector.tensor_copy(out=w1_grp[:], in_=w1_raw[:].rearrange("q t f -> q f t"))
+        nc.vector.tensor_copy(out=w_grp[:].rearrange("q (c i) t -> q c t i", i=4),
+                              in_=w_raw[:].rearrange("q t (c i) -> q c t i", i=4))
+        nc.vector.quantize_mx(out=w1_codes[:].bitcast(FP8X4), scales=w1_scl[:],
+                              in_=w1_grp[:].rearrange("q f t -> q (f t)"))
+        nc.vector.quantize_mx(out=w_codes[:].bitcast(FP8X4), scales=w_scl[:],
+                              in_=w_grp[:].rearrange("q d t -> q (d t)"))
 
         def consts_stage2():
-            b1_ps = psum.tile([P, D], F32, tag="mm2", bufs=1)
+            b1_ps = psum.tile([P, D], F32, tag="mm1", bufs=4)
             nc.tensor.matmul(out=b1_ps[:], lhsT=ones[:], rhs=crow[:, D:2 * D], start=True, stop=True)
-            gb_ps = psum.tile([P, P], BF16, tag="zt", bufs=3)
+            gb_ps = psum.tile([P, P], BF16, tag="mm2", bufs=1)
             nc.tensor.transpose(gb_ps[:], grow[:], ident_b[:])
-            nc.vector.tensor_copy(out=w1_grp[:], in_=w1_raw[:].rearrange("q t f -> q f t"))
-            nc.vector.tensor_copy(out=b1_sb[:], in_=b1_ps[:, 0:F].unsqueeze(1).to_broadcast([P, 4, F]))
-            nc.vector.tensor_copy(out=gb[:], in_=gb_ps[:, 0:8])
-            nc.vector.quantize_mx(out=w1_codes[:].bitcast(FP8X4), scales=w1_scl[:],
-                                  in_=w1_grp[:].rearrange("q f t -> q (f t)"))
+            nc.scalar.copy(out=b1_sb[:], in_=b1_ps[:, 0:F].unsqueeze(1).to_broadcast([P, 4, F]))
+            nc.scalar.copy(out=gb[:], in_=gb_ps[:, 0:8])
 
         def st_ta(u):
             n = SIZES[u]
             banks = []
             for h in range((n + 1) // 2):
                 m = min(2, n - 2 * h)
-                tpa = psum.tile([P, D], F32, tag="tpa", bufs=2)
+                tpa = psum.tile([P, D], F32, tag="tp", bufs=3)
                 for jj in range(m):
                     words = T["attn", u][:, 2 * h + jj, :].bitcast(F32)
                     for uu in range(2):
@@ -158,7 +155,7 @@ def tile_transformerblock_pb_t_kernel(tc, attn, x, w_out, b_out, ln2_g, ln2_b, w
             eng.tensor_tensor(out=T["xm", u][:, j, :], in0=T["x", u][:, j, :], in1=bo_sb[:], op=ALU.add)
 
         def st_m1(u, j):
-            mm1 = psum.tile([P, D], F32, tag="mm1", bufs=2)
+            mm1 = psum.tile([P, D], F32, tag="mm1", bufs=4)
             nc.tensor.matmul_mx(out=mm1[:], lhsT=T["a_codes", u][:, j * P:(j + 1) * P].bitcast(FP8X4),
                                 lhsT_scale=T["a_scl", u][:, j * P:(j + 1) * P],
                                 rhs=w_codes[:].bitcast(FP8X4), rhs_scale=w_scl[:], start=True, stop=True)
@@ -211,7 +208,7 @@ def tile_transformerblock_pb_t_kernel(tc, attn, x, w_out, b_out, ln2_g, ln2_b, w
             zt = None
             for t in range(4):
                 if t % per_bank == 0:
-                    zt = psum.tile([P, D], F32, tag="zt", bufs=3)
+                    zt = psum.tile([P, D], F32, tag="tp", bufs=3)
                 c0 = (t % per_bank) * n * P
                 for j in range(n):
                     nc.tensor.transpose(zt[:, c0 + j * P:c0 + (j + 1) * P], T["z", u][:, j, t * P:(t + 1) * P],
@@ -252,44 +249,47 @@ def tile_transformerblock_pb_t_kernel(tc, attn, x, w_out, b_out, ln2_g, ln2_b, w
             nc.scalar.activation(out=hid[:], in_=pre[:], func=ACT.Gelu)
             nc.sync.dma_start(out=hid_v[:, first[u]:first[u] + n, :], in_=hid[:])
 
-        for s in range(-CA_AHEAD, n_units + OE + 1):
+        for s in range(-CA_AHEAD, n_units + 4):
             if ok(s - 1):
                 st_pow(s - 1)
             if ok(s + XB_AHEAD):
                 st_xm(s + XB_AHEAD)
-                if s + XB_AHEAD not in XB_ON_VECTOR:
-                    for j in range(SIZES[s + XB_AHEAD] - 1):
-                        st_xb(s + XB_AHEAD, j, nc.gpsimd)
+                for j in range(SIZES[s + XB_AHEAD] - 1):
+                    st_xb(s + XB_AHEAD, j, nc.gpsimd)
+            nxt = SIZES[s + 1] if ok(s + 1) else 0
+            issued = 0
+            if nxt and not ok(s):
+                st_q1(s + 1)
             if ok(s):
-                for j in range(SIZES[s]):
-                    if s in XB_ON_VECTOR or j == SIZES[s] - 1:
+                n = SIZES[s]
+                for j in range(n):
+                    if j == n - 1:
                         st_xb(s, j, nc.vector)
                     st_a(s, j)
-                    if j + PRE < SIZES[s]:
-                        st_m1(s, j + PRE)
+                    if j == 0 and nxt:
+                        st_q1(s + 1)
+                    while issued < nxt and issued * n < (j + 1) * nxt:
+                        st_m1(s + 1, issued)
+                        issued += 1
                 st_nm(s)
-            if ok(s + 1):
-                st_q1(s + 1)
-                for j in range(min(PRE, SIZES[s + 1])):
-                    st_m1(s + 1, j)
-            if ok(s - OE):
-                st_m2(s - OE)
+            while issued < nxt:
+                st_m1(s + 1, issued)
+                issued += 1
             if ok(s):
                 st_b(s)
-            if s == 0:
-                consts_stage2()
-            if ok(s - OC):
-                st_c(s - OC)
-                st_tz_d(s - OC)
+            if ok(s - 1):
+                st_c(s - 1)
+                st_tz_d(s - 1)
             if ok(s + CA_AHEAD):
                 st_ta(s + CA_AHEAD)
-            if s == -CA_AHEAD:
-                consts_stage1()
-            if ok(s - OR):
-                st_r(s - OR)
-            if ok(s - OE):
-                st_e(s - OE)
-            if ok(s - OR):
-                st_q2(s - OR)
+            if s == -2:
+                consts_stage2()
+            if ok(s - 2):
+                st_r(s - 2)
+            if ok(s - 3):
+                st_e(s - 3)
+            if ok(s - 2):
+                st_q2(s - 2)
+                st_m2(s - 2)
             if ok(s + CA_AHEAD):
                 st_ca(s + CA_AHEAD)

@@ -170,9 +170,6 @@ def tile_transformerblock_pb_t_kernel(tc, attn, x, w_out, b_out, ln2_g, ln2_b, w
 
         def st_nm(u):
             n = SIZES[u]
-            negmean = work.tile([P, 4], F32, tag="negmean", bufs=4)
-            nc.vector.tensor_scalar_mul(out=negmean[:, 0:n], in0=T["sums", u][:, 0:n], scalar1=-1.0 / D)
-            T["negmean", u] = negmean
             nc.sync.dma_start(out=xmid_v[:, first[u]:first[u] + n, :], in_=T["xm", u][:])
 
         def st_b(u):
@@ -181,22 +178,36 @@ def tile_transformerblock_pb_t_kernel(tc, attn, x, w_out, b_out, ln2_g, ln2_b, w
             for j in range(SIZES[u]):
                 junk = work.tile([P, D], BF16, tag="junk", bufs=2)
                 nc.scalar.activation(out=junk[:], in_=T["xm", u][:, j, :], func=ACT.Square,
-                                     bias=T["negmean", u][:, j:j + 1], scale=1.0, accum_out=ssq[:, j:j + 1])
+                                     bias=T["sums", u][:, j:j + 1], scale=-1.0 * D, accum_out=ssq[:, j:j + 1])
 
         def st_pow(u):
             n = SIZES[u]
             var = work.tile([P, 4], F32, tag="var", bufs=4)
-            nc.gpsimd.tensor_scalar(out=var[:, 0:n], in0=T["ssq", u][:, 0:n], scalar1=1.0 / D, scalar2=EPS,
+            nc.gpsimd.tensor_scalar(out=var[:, 0:n], in0=T["ssq", u][:, 0:n], scalar1=1.0 / (D * D * D), scalar2=EPS,
                                     op0=ALU.mult, op1=ALU.add)
             rstd = work.tile([P, 4], F32, tag="rstd", bufs=4)
             nc.gpsimd.tensor_tensor(out=rstd[:, 0:n], in0=var[:, 0:n], in1=neghalf[:, 0:n], op=ALU.pow)
             T["rstd", u] = rstd
+            negmean = work.tile([P, 4], F32, tag="negmean", bufs=4)
+            nc.gpsimd.tensor_scalar(out=negmean[:, 0:n], in0=T["sums", u][:, 0:n], scalar1=-1.0 / D, scalar2=0.0,
+                                    op0=ALU.mult, op1=ALU.add)
+            T["negmean", u] = negmean
+            shift = work.tile([P, 4], F32, tag="shift", bufs=4)
+            nc.gpsimd.tensor_tensor(out=shift[:, 0:n], in0=negmean[:, 0:n], in1=rstd[:, 0:n], op=ALU.mult)
+            T["shift", u] = shift
 
-        def st_c(u):
+        def st_c_scalar(u):
             n = SIZES[u]
             z = work.tile([P, n, D], F32, tag="z", bufs=2)
             T["z", u] = z
-            for j in range(n):
+            for j in range(n // 2):
+                nc.scalar.activation(out=z[:, j, :], in_=T["xm", u][:, j, :], func=ACT.Identity,
+                                     bias=T["shift", u][:, j:j + 1], scale=T["rstd", u][:, j:j + 1])
+
+        def st_c(u):
+            n = SIZES[u]
+            z = T["z", u]
+            for j in range(n // 2, n):
                 nc.vector.tensor_scalar(out=z[:, j, :], in0=T["xm", u][:, j, :], scalar1=T["negmean", u][:, j:j + 1],
                                         scalar2=T["rstd", u][:, j:j + 1], op0=ALU.add, op1=ALU.mult)
 
@@ -275,6 +286,8 @@ def tile_transformerblock_pb_t_kernel(tc, attn, x, w_out, b_out, ln2_g, ln2_b, w
             while issued < nxt:
                 st_m1(s + 1, issued)
                 issued += 1
+            if ok(s - 1):
+                st_c_scalar(s - 1)
             if ok(s):
                 st_b(s)
             if ok(s - 1):

@@ -170,6 +170,9 @@ def tile_transformerblock_pb_t_kernel(tc, attn, x, w_out, b_out, ln2_g, ln2_b, w
 
         def st_nm(u):
             n = SIZES[u]
+            negmean = work.tile([P, 4], F32, tag="negmean", bufs=4)
+            nc.vector.tensor_scalar_mul(out=negmean[:, 0:n], in0=T["sums", u][:, 0:n], scalar1=-1.0 / D)
+            T["negmean", u] = negmean
             nc.sync.dma_start(out=xmid_v[:, first[u]:first[u] + n, :], in_=T["xm", u][:])
 
         def st_b(u):
@@ -178,36 +181,22 @@ def tile_transformerblock_pb_t_kernel(tc, attn, x, w_out, b_out, ln2_g, ln2_b, w
             for j in range(SIZES[u]):
                 junk = work.tile([P, D], BF16, tag="junk", bufs=2)
                 nc.scalar.activation(out=junk[:], in_=T["xm", u][:, j, :], func=ACT.Square,
-                                     bias=T["sums", u][:, j:j + 1], scale=-1.0 * D, accum_out=ssq[:, j:j + 1])
+                                     bias=T["negmean", u][:, j:j + 1], scale=1.0, accum_out=ssq[:, j:j + 1])
 
         def st_pow(u):
             n = SIZES[u]
             var = work.tile([P, 4], F32, tag="var", bufs=4)
-            nc.gpsimd.tensor_scalar(out=var[:, 0:n], in0=T["ssq", u][:, 0:n], scalar1=1.0 / (D * D * D), scalar2=EPS,
+            nc.gpsimd.tensor_scalar(out=var[:, 0:n], in0=T["ssq", u][:, 0:n], scalar1=1.0 / D, scalar2=EPS,
                                     op0=ALU.mult, op1=ALU.add)
             rstd = work.tile([P, 4], F32, tag="rstd", bufs=4)
             nc.gpsimd.tensor_tensor(out=rstd[:, 0:n], in0=var[:, 0:n], in1=neghalf[:, 0:n], op=ALU.pow)
             T["rstd", u] = rstd
-            negmean = work.tile([P, 4], F32, tag="negmean", bufs=4)
-            nc.gpsimd.tensor_scalar(out=negmean[:, 0:n], in0=T["sums", u][:, 0:n], scalar1=-1.0 / D, scalar2=0.0,
-                                    op0=ALU.mult, op1=ALU.add)
-            T["negmean", u] = negmean
-            shift = work.tile([P, 4], F32, tag="shift", bufs=4)
-            nc.gpsimd.tensor_tensor(out=shift[:, 0:n], in0=negmean[:, 0:n], in1=rstd[:, 0:n], op=ALU.mult)
-            T["shift", u] = shift
-
-        def st_c_scalar(u):
-            n = SIZES[u]
-            z = work.tile([P, n, D], F32, tag="z", bufs=2)
-            T["z", u] = z
-            for j in range(n // 2):
-                nc.scalar.activation(out=z[:, j, :], in_=T["xm", u][:, j, :], func=ACT.Identity,
-                                     bias=T["shift", u][:, j:j + 1], scale=T["rstd", u][:, j:j + 1])
 
         def st_c(u):
             n = SIZES[u]
-            z = T["z", u]
-            for j in range(n // 2, n):
+            z = work.tile([P, n, D], F32, tag="z", bufs=2)
+            T["z", u] = z
+            for j in range(n):
                 nc.vector.tensor_scalar(out=z[:, j, :], in0=T["xm", u][:, j, :], scalar1=T["negmean", u][:, j:j + 1],
                                         scalar2=T["rstd", u][:, j:j + 1], op0=ALU.add, op1=ALU.mult)
 
@@ -267,27 +256,17 @@ def tile_transformerblock_pb_t_kernel(tc, attn, x, w_out, b_out, ln2_g, ln2_b, w
                 st_xm(s + XB_AHEAD)
                 for j in range(SIZES[s + XB_AHEAD] - 1):
                     st_xb(s + XB_AHEAD, j, nc.gpsimd)
-            nxt = SIZES[s + 1] if ok(s + 1) else 0
-            issued = 0
-            if nxt and not ok(s):
-                st_q1(s + 1)
             if ok(s):
-                n = SIZES[s]
-                for j in range(n):
-                    if j == n - 1:
-                        st_xb(s, j, nc.vector)
+                for j in range(SIZES[s]):
                     st_a(s, j)
-                    if j == 0 and nxt:
-                        st_q1(s + 1)
-                    while issued < nxt and issued * n < (j + 1) * nxt:
-                        st_m1(s + 1, issued)
-                        issued += 1
+            if ok(s - 3):
+                st_e(s - 3)
+            if ok(s):
                 st_nm(s)
-            while issued < nxt:
-                st_m1(s + 1, issued)
-                issued += 1
-            if ok(s - 1):
-                st_c_scalar(s - 1)
+            if ok(s + 1):
+                st_q1(s + 1)
+                for j in range(SIZES[s + 1]):
+                    st_m1(s + 1, j)
             if ok(s):
                 st_b(s)
             if ok(s - 1):
@@ -299,8 +278,8 @@ def tile_transformerblock_pb_t_kernel(tc, attn, x, w_out, b_out, ln2_g, ln2_b, w
                 consts_stage2()
             if ok(s - 2):
                 st_r(s - 2)
-            if ok(s - 3):
-                st_e(s - 3)
+            if ok(s + 1):
+                st_xb(s + 1, SIZES[s + 1] - 1, nc.vector)
             if ok(s - 2):
                 st_q2(s - 2)
                 st_m2(s - 2)

from contextlib import ExitStack

import concourse.mybir as mybir
from concourse.masks import make_identity

F32 = mybir.dt.float32
BF16 = mybir.dt.bfloat16
U32 = mybir.dt.uint32
U8 = mybir.dt.uint8
FP8X4 = mybir.dt.float8_e4m3fn_x4
ALU = mybir.AluOpType
ACT = mybir.ActivationFunctionType

P = 128
TOK = 4096
D = 512
F = 128
NT = TOK // P
EPS = 1e-5

FLOPS = 2 * TOK * D * D + 2 * TOK * D * F

SIZES = (2, 4, 4, 4, 4, 4, 4, 4, 2)
MANUAL = True
CA_AHEAD = 3
XB_AHEAD = 2


def tile_transformerblock_pb_t_kernel(tc, attn, x, w_out, b_out, ln2_g, ln2_b, w1, b1, out_0, out_1):
    nc = tc.nc
    attn_v = attn.flatten_outer_dims().rearrange("(p n) k -> p n k", n=NT)
    x_v = x.flatten_outer_dims().rearrange("(p n) k -> p n k", n=NT)
    xmid_v = out_0.flatten_outer_dims().rearrange("(p n) k -> p n k", n=NT)
    hid_v = out_1.flatten_outer_dims().rearrange("(p n) k -> p n k", n=NT)
    n_units = len(SIZES)
    first = [sum(SIZES[:u]) for u in range(n_units)]
    assert sum(SIZES) == NT

    with ExitStack() as ctx:
        const = ctx.enter_context(tc.tile_pool(name="const", bufs=1))
        inp = ctx.enter_context(tc.tile_pool(name="inp", bufs=1))
        work = ctx.enter_context(tc.tile_pool(name="work", bufs=2))
        psum = ctx.enter_context(tc.psum_pool(name="psum", bufs=2))
        if MANUAL:
            ctx.enter_context(tc.manual_schedule())

        T = {}

        def ok(u):
            return 0 <= u < n_units

        ident_f = const.tile([P, P], F32)
        make_identity(nc, ident_f[:])
        ident_b = const.tile([P, P], BF16)
        make_identity(nc, ident_b[:])

        crow = const.tile([P, 2 * D], BF16)
        nc.vector.memset(crow[:], 0.0)
        grow = const.tile([P, P], BF16)
        nc.vector.memset(grow[:], 0.0)
        ones = const.tile([P, P], BF16)
        nc.vector.memset(ones[:], 1.0)
        neghalf = const.tile([P, 4], F32)
        nc.vector.memset(neghalf[:], -0.5)
        warm = const.tile([P, 2], F32)
        nc.vector.memset(warm[:], 0.0)
        nc.scalar.dma_start(out=crow[0:1, 0:D], in_=b_out.unsqueeze(0))
        w1_raw = const.tile([P, 4, F], BF16)
        nc.scalar.dma_start(out=w1_raw[:], in_=w1.rearrange("(t p) f -> p t f", p=P))
        nc.scalar.dma_start(out=crow[0:1, D:D + F], in_=b1.unsqueeze(0))
        nc.scalar.dma_start(out=grow[0:4, :], in_=ln2_g.rearrange("(t p) -> t p", p=P))
        nc.scalar.dma_start(out=grow[4:8, :], in_=ln2_b.rearrange("(t p) -> t p", p=P))
        nc.scalar.activation(out=warm[:, 1:2], in_=warm[:, 0:1], func=ACT.Gelu)

        w_raw = const.tile([P, 4, D], BF16)
        for u in range(n_units):
            n = SIZES[u]
            a_t = inp.tile([P, n, D], BF16, name="attn%d" % u)
            nc.sync.dma_start(out=a_t[:], in_=attn_v[:, first[u]:first[u] + n, :])
            T["attn", u] = a_t
            if u == 0:
                nc.sync.dma_start(
                    out=w_raw[:].rearrange("q (u e) d -> q u (e d)", u=2),
                    in_=w_out.rearrange("(u q e) d -> q u (e d)", u=2, e=2),
                )
            x_t = inp.tile([P, n, D], BF16, name="x%d" % u)
            nc.sync.dma_start(out=x_t[:], in_=x_v[:, first[u]:first[u] + n, :])
            T["x", u] = x_t

        w_grp = const.tile([P, D, 4], BF16, align_bytes=64)
        w_codes = const.tile([P, D], U32, align_bytes=64)
        w_scl = const.tile([P, D], U8, align_bytes=64)
        w1_grp = const.tile([P, F, 4], BF16, align_bytes=64)
        w1_codes = const.tile([P, F], U32, align_bytes=64)
        w1_scl = const.tile([P, F], U8, align_bytes=64)
        bo_sb = const.tile([P, D], F32)
        b1_sb = const.tile([P, 4, F], F32)
        gb = const.tile([P, 8], F32)

        bo_ps = psum.tile([P, D], F32, tag="mm1", bufs=4)
        nc.tensor.matmul(out=bo_ps[:], lhsT=ones[:], rhs=crow[:, 0:D], start=True, stop=True)
        nc.scalar.copy(out=bo_sb[:], in_=bo_ps[:])
        nc.vector.tensor_copy(out=w1_grp[:], in_=w1_raw[:].rearrange("q t f -> q f t"))
        nc.vector.tensor_copy(out=w_grp[:].rearrange("q (c i) t -> q c t i", i=4),
                              in_=w_raw[:].rearrange("q t (c i) -> q c t i", i=4))
        nc.vector.quantize_mx(out=w1_codes[:].bitcast(FP8X4), scales=w1_scl[:],
                              in_=w1_grp[:].rearrange("q f t -> q (f t)"))
        nc.vector.quantize_mx(out=w_codes[:].bitcast(FP8X4), scales=w_scl[:],
                              in_=w_grp[:].rearrange("q d t -> q (d t)"))

        def consts_stage2():
            b1_ps = psum.tile([P, D], F32, tag="mm1", bufs=4)
            nc.tensor.matmul(out=b1_ps[:], lhsT=ones[:], rhs=crow[:, D:2 * D], start=True, stop=True)
            gb_ps = psum.tile([P, P], BF16, tag="mm2", bufs=1)
            nc.tensor.transpose(gb_ps[:], grow[:], ident_b[:])
            nc.scalar.copy(out=b1_sb[:], in_=b1_ps[:, 0:F].unsqueeze(1).to_broadcast([P, 4, F]))
            nc.scalar.copy(out=gb[:], in_=gb_ps[:, 0:8])

        def st_ta(u):
            n = SIZES[u]
            banks = []
            for h in range((n + 1) // 2):
                m = min(2, n - 2 * h)
                tpa = psum.tile([P, D], F32, tag="tp", bufs=3)
                for jj in range(m):
                    words = T["attn", u][:, 2 * h + jj, :].bitcast(F32)
                    for uu in range(2):
                        c0 = (2 * jj + uu) * P
                        nc.tensor.transpose(tpa[:, c0:c0 + P], words[:, uu * P:(uu + 1) * P], ident_f[:])
                banks.append(tpa)
            T["tpa", u] = banks

        def st_ca(u):
            n = SIZES[u]
            grp1 = work.tile([P, n * P * 4], BF16, align_bytes=64, tag="grp1", bufs=3)
            T["grp1", u] = grp1
            g1f = grp1[:].bitcast(F32).rearrange("q (j r u) -> q j r u", j=n, u=2)
            for h in range((n + 1) // 2):
                m = min(2, n - 2 * h)
                nc.scalar.copy(out=g1f[:, 2 * h:2 * h + m, :, :],
                               in_=T["tpa", u][h][:, 0:m * 2 * P].rearrange("q (j u r) -> q j r u", j=m, u=2))

        def st_q1(u):
            n = SIZES[u]
            a_codes = work.tile([P, n * P], U32, align_bytes=64, tag="a_codes", bufs=3)
            a_scl = work.tile([P, n * P], U8, align_bytes=64, tag="a_scl", bufs=3)
            nc.vector.quantize_mx(out=a_codes[:].bitcast(FP8X4), scales=a_scl[:], in_=T["grp1", u][:])
            T["a_codes", u] = a_codes
            T["a_scl", u] = a_scl

        def st_xm(u):
            T["xm", u] = work.tile([P, SIZES[u], D], F32, tag="xm", bufs=5, name="xm")

        def st_xb(u, j, eng):
            eng.tensor_tensor(out=T["xm", u][:, j, :], in0=T["x", u][:, j, :], in1=bo_sb[:], op=ALU.add)

        def st_m1(u, j):
            mm1 = psum.tile([P, D], F32, tag="mm1", bufs=4)
            nc.tensor.matmul_mx(out=mm1[:], lhsT=T["a_codes", u][:, j * P:(j + 1) * P].bitcast(FP8X4),
                                lhsT_scale=T["a_scl", u][:, j * P:(j + 1) * P],
                                rhs=w_codes[:].bitcast(FP8X4), rhs_scale=w_scl[:], start=True, stop=True)
            T["mm1", u, j] = mm1

        def st_a(u, j):
            if j == 0:
                T["sums", u] = work.tile([P, 4], F32, tag="sums", bufs=4, name="sums")
            xm = T["xm", u]
            nc.vector.scalar_tensor_tensor(out=xm[:, j, :], in0=T["mm1", u, j][:], scalar=0.0, in1=xm[:, j, :],
                                           op0=ALU.add, op1=ALU.add, accum_out=T["sums", u][:, j:j + 1])

        def st_nm(u):
            n = SIZES[u]
            negmean = work.tile([P, 4], F32, tag="negmean", bufs=4)
            nc.vector.tensor_scalar_mul(out=negmean[:, 0:n], in0=T["sums", u][:, 0:n], scalar1=-1.0 / D)
            T["negmean", u] = negmean
            nc.sync.dma_start(out=xmid_v[:, first[u]:first[u] + n, :], in_=T["xm", u][:])

        def st_b(u):
            ssq = work.tile([P, 4], F32, tag="ssq", bufs=4)
            T["ssq", u] = ssq
            for j in range(SIZES[u]):
                junk = work.tile([P, D], BF16, tag="junk", bufs=2)
                nc.scalar.activation(out=junk[:], in_=T["xm", u][:, j, :], func=ACT.Square,
                                     bias=T["negmean", u][:, j:j + 1], scale=1.0, accum_out=ssq[:, j:j + 1])

        def st_pow(u):
            n = SIZES[u]
            var = work.tile([P, 4], F32, tag="var", bufs=4)
            nc.gpsimd.tensor_scalar(out=var[:, 0:n], in0=T["ssq", u][:, 0:n], scalar1=1.0 / D, scalar2=EPS,
                                    op0=ALU.mult, op1=ALU.add)
            rstd = work.tile([P, 4], F32, tag="rstd", bufs=4)
            nc.gpsimd.tensor_tensor(out=rstd[:, 0:n], in0=var[:, 0:n], in1=neghalf[:, 0:n], op=ALU.pow)
            T["rstd", u] = rstd

        def st_c(u):
            n = SIZES[u]
            z = work.tile([P, n, D], F32, tag="z", bufs=2)
            T["z", u] = z
            for j in range(n):
                nc.vector.tensor_scalar(out=z[:, j, :], in0=T["xm", u][:, j, :], scalar1=T["negmean", u][:, j:j + 1],
                                        scalar2=T["rstd", u][:, j:j + 1], op0=ALU.add, op1=ALU.mult)

        def st_tz_d(u):
            n = SIZES[u]
            per_bank = 4 // n
            planes = work.tile([P, 4, n * P], BF16, tag="planes", bufs=2)
            T["planes", u] = planes
            zt = None
            for t in range(4):
                if t % per_bank == 0:
                    zt = psum.tile([P, D], F32, tag="tp", bufs=3)
                c0 = (t % per_bank) * n * P
                for j in range(n):
                    nc.tensor.transpose(zt[:, c0 + j * P:c0 + (j + 1) * P], T["z", u][:, j, t * P:(t + 1) * P],
                                        ident_f[:])
                nc.scalar.activation(out=planes[:, t, :], in_=zt[:, c0:c0 + n * P], func=ACT.Identity,
                                     bias=gb[:, 4 + t:5 + t], scale=gb[:, t:t + 1])

        def st_r(u):
            n = SIZES[u]
            grp2 = work.tile([P, n * P, 4], BF16, align_bytes=64, tag="grp2", bufs=2)
            T["grp2", u] = grp2
            nc.vector.tensor_copy(out=grp2[:].rearrange("p (c i) t -> p c t i", i=4),
                                  in_=T["planes", u][:].rearrange("p t (c i) -> p c t i", i=4))

        def st_q2(u):
            n = SIZES[u]
            h_codes = work.tile([P, n * P], U32, align_bytes=64, tag="h_codes", bufs=2)
            h_scl = work.tile([P, n * P], U8, align_bytes=64, tag="h_scl", bufs=2)
            nc.vector.quantize_mx(out=h_codes[:].bitcast(FP8X4), scales=h_scl[:],
                                  in_=T["grp2", u][:].rearrange("p r t -> p (r t)"))
            T["h_codes", u] = h_codes
            T["h_scl", u] = h_scl

        def st_m2(u):
            n = SIZES[u]
            mm2 = psum.tile([P, n, F], F32, tag="mm2", bufs=1)
            T["mm2", u] = mm2
            for j in range(n):
                nc.tensor.matmul_mx(out=mm2[:, j, :], lhsT=T["h_codes", u][:, j * P:(j + 1) * P].bitcast(FP8X4),
                                    lhsT_scale=T["h_scl", u][:, j * P:(j + 1) * P],
                                    rhs=w1_codes[:].bitcast(FP8X4), rhs_scale=w1_scl[:], start=True, stop=True)

        def st_e(u):
            n = SIZES[u]
            pre = work.tile([P, n, F], F32, tag="pre", bufs=2)
            nc.vector.tensor_tensor(out=pre[:], in0=T["mm2", u][:], in1=b1_sb[:, 0:n, :], op=ALU.add)
            hid = work.tile([P, n, F], F32, tag="hid", bufs=3)
            nc.scalar.activation(out=hid[:], in_=pre[:], func=ACT.Gelu)
            nc.sync.dma_start(out=hid_v[:, first[u]:first[u] + n, :], in_=hid[:])

        for s in range(-CA_AHEAD, n_units + 4):
            if ok(s - 1):
                st_pow(s - 1)
            if ok(s + XB_AHEAD):
                st_xm(s + XB_AHEAD)
                for j in range(SIZES[s + XB_AHEAD] - 1):
                    st_xb(s + XB_AHEAD, j, nc.gpsimd)
            if ok(s):
                for j in range(SIZES[s]):
                    st_a(s, j)
            if ok(s - 3):
                st_e(s - 3)
            if ok(s):
                st_nm(s)
            if ok(s + 1):
                st_q1(s + 1)
                for j in range(SIZES[s + 1]):
                    st_m1(s + 1, j)
            if ok(s):
                st_b(s)
            if ok(s - 1):
                st_c(s - 1)
                st_tz_d(s - 1)
            if ok(s + CA_AHEAD):
                st_ta(s + CA_AHEAD)
            if s == -2:
                consts_stage2()
            if ok(s - 2):
                st_r(s - 2)
            if ok(s + 1):
                st_xb(s + 1, SIZES[s + 1] - 1, nc.vector)
            if ok(s - 2):
                st_q2(s - 2)
                st_m2(s - 2)
            if ok(s + CA_AHEAD):
                st_ca(s + CA_AHEAD)
